import numpy as np
import ml_dtypes


def mxq(x, axis, fmt="e4m3"):
    dtype, down = {"e4m3": (ml_dtypes.float8_e4m3fn, 7), "e5m2": (ml_dtypes.float8_e5m2, 14)}[fmt]
    v = np.moveaxis(np.asarray(x, np.float32).astype(ml_dtypes.bfloat16).astype(np.float64), axis, -1)
    blocks = v.reshape(v.shape[:-1] + (-1, 32))
    amax = np.abs(blocks).max(-1, keepdims=True)
    byte = np.maximum(np.where(amax > 0, np.frexp(amax)[1] - 1 + 127, 0) - down, 1)
    scale = np.exp2(byte - 127.0)
    codes = (blocks / scale).astype(np.float32).astype(dtype).astype(np.float64)
    return np.moveaxis((codes * scale).reshape(v.shape), -1, axis)


WIDE = False


def mx_kscale(k):
    if not WIDE:
        return np.ones(k)
    levels = np.array([10, -10, 5, -5, 0])
    if k % 512:
        return np.exp2(np.random.permutation(np.resize(levels, k // 32))).repeat(32)
    a = np.empty((k // 512, 16))
    for p in range(k // 512):
        a[p, :8] = np.random.permutation(np.resize(levels, 8))
        for g in range(8):
            far = levels[np.abs(levels - a[p, g]) >= 10]
            a[p, g + 8] = far[np.random.randint(len(far))]
    return np.exp2(a.ravel()).repeat(32)


BF16 = ml_dtypes.bfloat16


def bf(x):
    return np.asarray(x, np.float32).astype(BF16)


def f64(x):
    return np.asarray(x).astype(np.float64)


B, T, D, H, DH, R, F = 2, 4096, 512, 2, 128, 32, 4096
EPS = 1e-5
E = H * DH


def rope(u, c, s):
    ur, up = u[..., :R], u[..., R:]
    c = c[None, :, None, :]
    s = s[None, :, None, :]
    ue, uo = ur[..., ::2], ur[..., 1::2]
    ur2 = np.stack([ue * c - uo * s, uo * c + ue * s], axis=-1).reshape(ur.shape)
    return np.concatenate([ur2, up], axis=-1)


def setup_inputs():
    rn = np.random.standard_normal
    s = mx_kscale(D)
    ang = np.random.uniform(0.0, 2.0 * np.pi, (T, R // 2))
    return {
        "x": bf(3.0 * np.sqrt(EPS) * (rn((B, T, D)) + 0.5 * rn((B, T, 1)))),
        "ln_scale": bf((1.0 + 0.1 * rn(D)) * s),
        "ln_offset": bf(0.1 * rn(D) * s),
        "wq": bf(rn((D, E)) / np.sqrt(D) / s[:, None]),
        "wk": bf(rn((D, E)) / np.sqrt(D) / s[:, None]),
        "wv": bf(rn((D, E)) / np.sqrt(D) / s[:, None]),
        "rope_cos": bf(np.cos(ang)),
        "rope_sin": bf(np.sin(ang)),
    }


def reference(x, ln_scale, ln_offset, wq, wk, wv, rope_cos, rope_sin):
    x = f64(x)
    mean = x.mean(-1, keepdims=True)
    var = ((x - mean) ** 2).mean(-1, keepdims=True)
    xn = (x - mean) * (1.0 / np.sqrt(var + EPS))
    xn = xn * f64(ln_scale) + f64(ln_offset)
    xq = mxq(xn, 2, "e4m3")
    q = (xq @ mxq(f64(wq), 0, "e4m3")).reshape(B, T, H, DH)
    k = (xq @ mxq(f64(wk), 0, "e4m3")).reshape(B, T, H, DH)
    v = (xq @ mxq(f64(wv), 0, "e4m3")).reshape(B, T, H, DH)
    c, s = f64(rope_cos), f64(rope_sin)
    return rope(q, c, s), rope(k, c, s), v

@@ -1,0 +1,352 @@
+from contextlib import ExitStack
+
+import concourse.mybir as mybir
+from concourse.masks import make_identity
+
+F32 = mybir.dt.float32
+BF16 = mybir.dt.bfloat16
+U32 = mybir.dt.uint32
+U8 = mybir.dt.uint8
+FP8X4 = mybir.dt.float8_e4m3fn_x4
+ALU = mybir.AluOpType
+ACT = mybir.ActivationFunctionType
+
+P = 128
+PACK = 4
+BANK = 512
+BANKS = 8
+B, T, D, H, DH, ROT = 2, 4096, 512, 2, 128, 32
+E = H * DH
+EPS = 1e-5
+TOKENS = B * T
+TILES = 4
+MACRO = P * TILES
+N_MACRO = TOKENS // MACRO
+POS_MACRO = T // MACRO
+HALF = ROT // 2
+HEADS_QK = 2 * H
+
+ROPE_COLS = 2 * HEADS_QK * ROT
+V_COLS = E
+PASS_COLS = HEADS_QK * (DH - ROT)
+ROPE_AT = 0
+V_AT = ROPE_AT + ROPE_COLS
+PASS_AT = V_AT + V_COLS
+W_COLS = PASS_AT + PASS_COLS
+
+FLOPS = 2 * TOKENS * D * 3 * E
+
+LOAD_AHEAD = 6
+STATS_AHEAD = 4
+NORM_AHEAD = 3
+PLANES_AHEAD = 2
+QUANT_AHEAD = 1
+
+GPSIMD_TILES = 3
+
+
+def tile_transformerlayershard_pa_t_kernel(
+    tc, x, ln_scale, ln_offset, wq, wk, wv, rope_cos, rope_sin, out_0, out_1, out_2
+):
+    nc = tc.nc
+    x_rows = x.rearrange("b t k -> (b t) k").rearrange("(m p i) k -> m p (i k)", p=P, i=TILES)
+    out_rows = [
+        o.rearrange("b t h d -> (b t) (h d)").rearrange("(m p i) c -> m p (i c)", p=P, i=TILES)
+        for o in (out_0, out_1, out_2)
+    ]
+
+    with ExitStack() as ctx:
+        const = ctx.enter_context(tc.tile_pool(name="const", bufs=1))
+        x_pool = ctx.enter_context(tc.tile_pool(name="x", bufs=5))
+        small = ctx.enter_context(tc.tile_pool(name="small", bufs=4))
+        z_pool = ctx.enter_context(tc.tile_pool(name="z", bufs=3))
+        work = ctx.enter_context(tc.tile_pool(name="work", bufs=2))
+        out_pool = ctx.enter_context(tc.tile_pool(name="out", bufs=3))
+        psum = ctx.enter_context(tc.psum_pool(name="psum", bufs=BANKS))
+        ctx.enter_context(tc.manual_schedule())
+
+        def bank(name):
+            return psum.tile([P, BANK], F32, tag="bank", name=name)
+
+        x_of, stats_of, mean_var_of, std_of, rstd_of, neg_mean_of, shift_of = {}, {}, {}, {}, {}, {}, {}
+        z_of, planes_ps_of, planes_of, grouped_of, codes_of, scales_of = {}, {}, {}, {}, {}, {}
+        banks_of, stage_of, products_of = {}, {}, {}
+
+        def load(m):
+            x_of[m] = x_pool.tile([P, TILES, D], BF16, name="x_sb")
+            nc.sync.dma_start(out=x_of[m][:].rearrange("p i k -> p (i k)"), in_=x_rows[m])
+
+        load(0)
+
+        affine_raw = []
+        for c, vec in enumerate((ln_scale, ln_offset)):
+            raw = const.tile([P, PACK], BF16, name="affine_raw%d" % c)
+            nc.scalar.dma_start(out=raw[:], in_=vec.rearrange("(p j) -> p j", j=PACK))
+            affine_raw.append(raw)
+        rot_raw = []
+        for c, table in enumerate((rope_cos, rope_sin)):
+            raw = const.tile([P, POS_MACRO, TILES * HALF], BF16, name="rot_raw%d" % c)
+            nc.scalar.dma_start(out=raw[:], in_=table.rearrange("(m p i) a -> p m (i a)", p=P, i=TILES))
+            rot_raw.append(raw)
+
+        w_raw = []
+        for o, w in enumerate((wq, wk, wv)):
+            w_sb = const.tile([P, PACK, E], BF16, name="w_raw%d" % o)
+            nc.sync.dma_start(out=w_sb[:], in_=w.rearrange("(p j) n -> p j n", j=PACK))
+            w_raw.append(w_sb)
+
+        one_col = const.tile([P, 1], F32)
+        nc.vector.memset(one_col[:], 1.0)
+        first_sqrt = const.tile([P, 1], F32)
+        nc.scalar.activation(out=first_sqrt[:], in_=one_col[:], func=ACT.Sqrt)
+        eps_col = const.tile([P, 1], F32)
+        nc.vector.tensor_scalar(out=eps_col[:], in0=one_col[:], scalar1=EPS, scalar2=None, op0=ALU.mult)
+
+        ident = const.tile([P, P], F32)
+        make_identity(nc, ident[:])
+
+        affine = const.tile([P, 2 * PACK], F32)
+        for c in range(2):
+            nc.scalar.copy(out=affine[:, c * PACK : (c + 1) * PACK], in_=affine_raw[c][:])
+
+        rot = const.tile([P, POS_MACRO * TILES, 2, ROT], F32)
+        for c in range(2):
+            nc.gpsimd.tensor_scalar(
+                out=rot[:, :, c, :].rearrange("p t (a e) -> p t a e", e=2),
+                in0=rot_raw[c][:]
+                .rearrange("p m (i a) -> p (m i) a", a=HALF)
+                .unsqueeze(3)
+                .to_broadcast([P, POS_MACRO * TILES, HALF, 2]),
+                scalar1=1.0,
+                scalar2=0.0,
+                op0=ALU.mult,
+                op1=ALU.add,
+            )
+
+        w_grouped = const.tile([P, W_COLS, PACK], BF16, align_bytes=64)
+        w_codes = const.tile([P, W_COLS], U32, align_bytes=64)
+        w_scales = const.tile([P, W_COLS], U8, align_bytes=64)
+
+        def regroup_weights(o):
+            if o == 2:
+                nc.vector.tensor_copy(
+                    out=w_grouped[:, V_AT : V_AT + V_COLS, :], in_=w_raw[2][:].rearrange("p j n -> p n j")
+                )
+                return
+            by_col = w_raw[o][:].rearrange("p j (h d) -> p h d j", h=H)
+            head_cols = H * ROT
+            plain_at = ROPE_AT + o * head_cols
+            nc.vector.tensor_copy(
+                out=w_grouped[:, plain_at : plain_at + head_cols, :].rearrange("p (h f) j -> p h f j", h=H),
+                in_=by_col[:, :, 0:ROT, :],
+            )
+            swap_at = ROPE_AT + HEADS_QK * ROT + o * head_cols
+            swapped = w_grouped[:, swap_at : swap_at + head_cols, :].rearrange("p (h a e) j -> p h a e j", h=H, e=2)
+            pairs = by_col[:, :, 0:ROT, :].rearrange("p h (a e) j -> p h a e j", e=2)
+            nc.vector.tensor_scalar(
+                out=swapped[:, :, :, 0, :], in0=pairs[:, :, :, 1, :], scalar1=-1.0, scalar2=None, op0=ALU.mult
+            )
+            nc.vector.tensor_copy(out=swapped[:, :, :, 1, :], in_=pairs[:, :, :, 0, :])
+            pass_cols = H * (DH - ROT)
+            pass_at = PASS_AT + o * pass_cols
+            nc.vector.tensor_copy(
+                out=w_grouped[:, pass_at : pass_at + pass_cols, :].rearrange("p (h d) j -> p h d j", h=H),
+                in_=by_col[:, :, ROT:DH, :],
+            )
+
+        def quantise_weights():
+            for lo, hi in ((0, 512), (512, 768), (768, 896)):
+                nc.vector.quantize_mx(
+                    out=w_codes[:, lo:hi].bitcast(FP8X4),
+                    scales=w_scales[:, lo:hi],
+                    in_=w_grouped[:, lo:hi, :].rearrange("p c j -> p (c j)"),
+                )
+
+        def token_stats(m, i):
+            if i == 0:
+                stats_of[m] = small.tile([P, TILES, 6], F32, name="stats")
+            nc.vector.bn_stats(out=stats_of[m][:, i, :], in_=x_of[m][:, i, :])
+
+        def mean_and_variance(m):
+            mean_var_of[m] = small.tile([P, TILES, 2], F32, name="mean_var")
+            for i in range(TILES):
+                nc.vector.bn_aggr(out=mean_var_of[m][:, i, :], in_=stats_of[m][:, i, :])
+
+        def std_dev(m):
+            std_of[m] = small.tile([P, TILES], F32, name="std")
+            nc.scalar.activation(out=std_of[m][:], in_=mean_var_of[m][:, :, 1], func=ACT.Sqrt, bias=eps_col[:])
+
+        def negate_mean(m):
+            neg_mean_of[m] = small.tile([P, TILES], F32, name="neg_mean")
+            nc.gpsimd.tensor_scalar(
+                out=neg_mean_of[m][:], in0=mean_var_of[m][:, :, 0], scalar1=-1.0, scalar2=0.0, op0=ALU.mult, op1=ALU.add
+            )
+
+        def inverse_std(m):
+            rstd_of[m] = small.tile([P, TILES], F32, name="rstd")
+            nc.vector.reciprocal(out=rstd_of[m][:], in_=std_of[m][:])
+
+        def normalise_on_gpsimd(m):
+            z_of[m] = z_pool.tile([P, TILES, PACK, P], F32, name="z")
+            shift_of[m] = small.tile([P, TILES - GPSIMD_TILES], F32, name="shift")
+            nc.gpsimd.tensor_tensor(
+                out=shift_of[m][:],
+                in0=neg_mean_of[m][:, GPSIMD_TILES:TILES],
+                in1=rstd_of[m][:, GPSIMD_TILES:TILES],
+                op=ALU.mult,
+            )
+            for i in range(GPSIMD_TILES):
+                nc.gpsimd.tensor_scalar(
+                    out=z_of[m][:, i, :, :],
+                    in0=x_of[m][:, i, :].rearrange("p (c j) -> p j c", j=PACK),
+                    scalar1=neg_mean_of[m][:, i : i + 1],
+                    scalar2=rstd_of[m][:, i : i + 1],
+                    op0=ALU.add,
+                    op1=ALU.mult,
+                )
+
+        def normalise_on_scalar(m):
+            for i in range(GPSIMD_TILES, TILES):
+                nc.scalar.activation(
+                    out=z_of[m][:, i, :, :],
+                    in_=x_of[m][:, i, :].rearrange("p (c j) -> p j c", j=PACK),
+                    func=ACT.Identity,
+                    scale=rstd_of[m][:, i : i + 1],
+                    bias=shift_of[m][:, i - GPSIMD_TILES : i - GPSIMD_TILES + 1],
+                )
+
+        def transpose(m):
+            planes_ps_of[m] = [bank("plane_ps%d" % j) for j in range(PACK)]
+            for j in range(PACK):
+                for i in range(TILES):
+                    nc.tensor.transpose(
+                        planes_ps_of[m][j][:, i * P : (i + 1) * P], z_of[m][:, i, j, :], ident[:]
+                    )
+
+        def scale_shift(m):
+            planes_of[m] = work.tile([P, PACK, MACRO], BF16, name="xn_planes")
+            for j in range(PACK):
+                nc.scalar.activation(
+                    out=planes_of[m][:, j, :],
+                    in_=planes_ps_of[m][j][:],
+                    func=ACT.Identity,
+                    scale=affine[:, j : j + 1],
+                    bias=affine[:, PACK + j : PACK + j + 1],
+                )
+
+        def regroup(m):
+            grouped_of[m] = work.tile([P, MACRO, PACK], BF16, align_bytes=64, name="xn_grouped")
+            nc.vector.tensor_copy(
+                out=grouped_of[m][:].rearrange("p (c r) j -> p c j r", r=4),
+                in_=planes_of[m][:].rearrange("p j (c r) -> p c j r", r=4),
+            )
+
+        def quantise(m):
+            codes_of[m] = work.tile([P, MACRO], U32, align_bytes=64, name="xn_codes")
+            scales_of[m] = work.tile([P, MACRO], U8, align_bytes=64, name="xn_scales")
+            nc.vector.quantize_mx(
+                out=codes_of[m][:].bitcast(FP8X4),
+                scales=scales_of[m][:],
+                in_=grouped_of[m][:].rearrange("p t j -> p (t j)"),
+            )
+
+        def one_pass(m, i, out_ps, at, cols):
+            nc.tensor.matmul_mx(
+                out=out_ps,
+                lhsT=codes_of[m][:, i * P : (i + 1) * P].bitcast(FP8X4),
+                lhsT_scale=scales_of[m][:, i * P : (i + 1) * P],
+                rhs=w_codes[:, at : at + cols].bitcast(FP8X4),
+                rhs_scale=w_scales[:, at : at + cols],
+                start=True,
+                stop=True,
+            )
+
+        def project(m, pair):
+            first = 2 * pair
+            rope_ps = bank("rope_ps")
+            v_ps = bank("v_ps")
+            pass_ps = [bank("pass_ps%d" % n) for n in range(2)]
+            banks_of[(m, pair)] = (v_ps, pass_ps, rope_ps)
+            for n in range(2):
+                one_pass(m, first + n, rope_ps[:, n * ROPE_COLS : (n + 1) * ROPE_COLS], ROPE_AT, ROPE_COLS)
+            for n in range(2):
+                one_pass(m, first + n, v_ps[:, n * V_COLS : (n + 1) * V_COLS], V_AT, V_COLS)
+            for n in range(2):
+                one_pass(m, first + n, pass_ps[n][:, 0:256], PASS_AT, 256)
+                one_pass(m, first + n, pass_ps[n][:, 256:PASS_COLS], PASS_AT + 256, PASS_COLS - 256)
+
+        def copy_out(m, pair):
+            first = 2 * pair
+            if pair == 0:
+                stage_of[m] = out_pool.tile([P, 3, TILES, E], F32, name="stage")
+            stage = stage_of[m]
+            v_ps, pass_ps, rope_ps = banks_of[(m, pair)]
+            nc.scalar.copy(out=stage[:, 2, first : first + 2, :].rearrange("p i c -> p (i c)"), in_=v_ps[:])
+            for n in range(2):
+                nc.scalar.copy(
+                    out=stage[:, 0:2, first + n, :].rearrange("p o (h d) -> p o h d", h=H)[:, :, :, ROT:DH],
+                    in_=pass_ps[n][:, 0:PASS_COLS].rearrange("p (o h d) -> p o h d", o=2, h=H),
+                )
+
+        def rope_products(m, pair):
+            first = 2 * pair
+            if pair == 0:
+                products_of[m] = out_pool.tile([P, TILES, 2, HEADS_QK, ROT], F32, name="products")
+            v_ps, pass_ps, rope_ps = banks_of[(m, pair)]
+            pos = (m % POS_MACRO) * TILES + first
+            nc.vector.tensor_tensor(
+                out=products_of[m][:, first : first + 2, :, :, :].rearrange("p i c g f -> p (i c) g f"),
+                in0=rope_ps[:].rearrange("p (a g f) -> p a g f", g=HEADS_QK, f=ROT),
+                in1=rot[:, pos : pos + 2, :, :]
+                .rearrange("p i c f -> p (i c) f")
+                .unsqueeze(2)
+                .to_broadcast([P, 4, HEADS_QK, ROT]),
+                op=ALU.mult,
+            )
+
+        def store(m, o):
+            nc.sync.dma_start(out=out_rows[o][m], in_=stage_of[m][:, o, :, :].rearrange("p i c -> p (i c)"))
+
+        def rotate_and_store(m):
+            for o in range(2):
+                nc.gpsimd.tensor_tensor(
+                    out=stage_of[m][:, o, :, :].rearrange("p i (h d) -> p i h d", h=H)[:, :, :, 0:ROT],
+                    in0=products_of[m][:, :, 0, o * H : (o + 1) * H, :],
+                    in1=products_of[m][:, :, 1, o * H : (o + 1) * H, :],
+                    op=ALU.add,
+                )
+                store(m, o)
+
+        def when(m, stage, *args):
+            if 0 <= m < N_MACRO:
+                stage(m, *args)
+
+        for s in range(-LOAD_AHEAD, N_MACRO + 1):
+            if s + LOAD_AHEAD > 0:
+                when(s + LOAD_AHEAD, load)
+            when(s + NORM_AHEAD, std_dev)
+            when(s + NORM_AHEAD, negate_mean)
+            when(s - 1, rotate_and_store)
+            when(s + QUANT_AHEAD, regroup)
+            when(s, rope_products, 0)
+            when(s, copy_out, 0)
+            when(s, project, 1)
+            when(s + QUANT_AHEAD, quantise)
+            when(s + NORM_AHEAD, inverse_std)
+            when(s + NORM_AHEAD, normalise_on_gpsimd)
+            when(s + STATS_AHEAD, token_stats, 0)
+            when(s + STATS_AHEAD, token_stats, 1)
+            when(s + PLANES_AHEAD, scale_shift)
+            when(s + QUANT_AHEAD, project, 0)
+            when(s + STATS_AHEAD, token_stats, 2)
+            when(s + NORM_AHEAD, normalise_on_scalar)
+            when(s, rope_products, 1)
+            when(s, copy_out, 1)
+            when(s, store, 2)
+            when(s + NORM_AHEAD, transpose)
+            when(s + STATS_AHEAD, token_stats, 3)
+            when(s + STATS_AHEAD, mean_and_variance)
+            if 0 <= s + STATS_AHEAD < 3:
+                regroup_weights(s + STATS_AHEAD)
+            if s + PLANES_AHEAD == 0:
+                quantise_weights()

@@ -36,13 +36,20 @@ W_COLS = PASS_AT + PASS_COLS
 
 FLOPS = 2 * TOKENS * D * 3 * E
 
-LOAD_AHEAD = 6
-STATS_AHEAD = 4
-NORM_AHEAD = 3
-PLANES_AHEAD = 2
-QUANT_AHEAD = 1
+UNITS = (
+    [(0, 0, 1), (0, 1, 1), (0, 2, 2)]
+    + [(m, 0, TILES) for m in range(1, N_MACRO - 1)]
+    + [(N_MACRO - 1, 0, 2), (N_MACRO - 1, 2, 1), (N_MACRO - 1, 3, 1)]
+)
 
-GPSIMD_TILES = 3
+STATS_AHEAD = 5
+NORM_AHEAD = 4
+TRANSPOSE_AHEAD = 3
+PLANES_AHEAD = 2
+GROUP_AHEAD = 1
+
+SCALAR_NORM_UNITS = 9
+VECTOR_COPY_FROM = len(UNITS) - 5
 
 
 def tile_transformerlayershard_pa_t_kernel(
@@ -57,7 +64,6 @@ def tile_transformerlayershard_pa_t_kernel(
 
     with ExitStack() as ctx:
         const = ctx.enter_context(tc.tile_pool(name="const", bufs=1))
-        x_pool = ctx.enter_context(tc.tile_pool(name="x", bufs=5))
         small = ctx.enter_context(tc.tile_pool(name="small", bufs=4))
         z_pool = ctx.enter_context(tc.tile_pool(name="z", bufs=3))
         work = ctx.enter_context(tc.tile_pool(name="work", bufs=2))
@@ -68,37 +74,40 @@ def tile_transformerlayershard_pa_t_kernel(
         def bank(name):
             return psum.tile([P, BANK], F32, tag="bank", name=name)
 
-        x_of, stats_of, mean_var_of, std_of, rstd_of, neg_mean_of, shift_of = {}, {}, {}, {}, {}, {}, {}
+        x_of, stats_of, mean_var_of, rstd_of, neg_mean_of = {}, {}, {}, {}, {}
         z_of, planes_ps_of, planes_of, grouped_of, codes_of, scales_of = {}, {}, {}, {}, {}, {}
         banks_of, stage_of, products_of = {}, {}, {}
 
-        def load(m):
-            x_of[m] = x_pool.tile([P, TILES, D], BF16, name="x_sb")
-            nc.sync.dma_start(out=x_of[m][:].rearrange("p i k -> p (i k)"), in_=x_rows[m])
+        def load(u):
+            m, i0, n = UNITS[u]
+            x_of[u] = const.tile([P, n, D], BF16, name="x_sb%d" % u)
+            nc.sync.dma_start(out=x_of[u][:].rearrange("p i k -> p (i k)"), in_=x_rows[m][:, i0 * D : (i0 + n) * D])
 
         load(0)
+        load(1)
 
         affine_raw = []
         for c, vec in enumerate((ln_scale, ln_offset)):
             raw = const.tile([P, PACK], BF16, name="affine_raw%d" % c)
             nc.scalar.dma_start(out=raw[:], in_=vec.rearrange("(p j) -> p j", j=PACK))
             affine_raw.append(raw)
-        rot_raw = []
-        for c, table in enumerate((rope_cos, rope_sin)):
-            raw = const.tile([P, POS_MACRO, TILES * HALF], BF16, name="rot_raw%d" % c)
-            nc.scalar.dma_start(out=raw[:], in_=table.rearrange("(m p i) a -> p m (i a)", p=P, i=TILES))
-            rot_raw.append(raw)
-
         w_raw = []
         for o, w in enumerate((wq, wk, wv)):
             w_sb = const.tile([P, PACK, E], BF16, name="w_raw%d" % o)
             nc.sync.dma_start(out=w_sb[:], in_=w.rearrange("(p j) n -> p j n", j=PACK))
             w_raw.append(w_sb)
+        rot_raw = []
+        for c, table in enumerate((rope_cos, rope_sin)):
+            raw = const.tile([P, POS_MACRO, TILES * HALF], BF16, name="rot_raw%d" % c)
+            nc.scalar.dma_start(out=raw[:], in_=table.rearrange("(m p i) a -> p m (i a)", p=P, i=TILES))
+            rot_raw.append(raw)
+        for u in range(2, len(UNITS)):
+            load(u)
 
         one_col = const.tile([P, 1], F32)
         nc.vector.memset(one_col[:], 1.0)
-        first_sqrt = const.tile([P, 1], F32)
-        nc.scalar.activation(out=first_sqrt[:], in_=one_col[:], func=ACT.Sqrt)
+        first_act = const.tile([P, 1], F32)
+        nc.scalar.activation(out=first_act[:], in_=one_col[:], func=ACT.Abs_reciprocal_sqrt)
         eps_col = const.tile([P, 1], F32)
         nc.vector.tensor_scalar(out=eps_col[:], in0=one_col[:], scalar1=EPS, scalar2=None, op0=ALU.mult)
 
@@ -109,47 +118,58 @@ def tile_transformerlayershard_pa_t_kernel(
         for c in range(2):
             nc.scalar.copy(out=affine[:, c * PACK : (c + 1) * PACK], in_=affine_raw[c][:])
 
-        rot = const.tile([P, POS_MACRO * TILES, 2, ROT], F32)
-        for c in range(2):
-            nc.gpsimd.tensor_scalar(
-                out=rot[:, :, c, :].rearrange("p t (a e) -> p t a e", e=2),
-                in0=rot_raw[c][:]
+        rot = const.tile([P, POS_MACRO * TILES, 2, H, ROT], F32)
+
+        def rotation_views(c, h):
+            return (
+                rot[:, :, c, h, :].rearrange("p t (a e) -> p t a e", e=2),
+                rot_raw[c][:]
                 .rearrange("p m (i a) -> p (m i) a", a=HALF)
                 .unsqueeze(3)
                 .to_broadcast([P, POS_MACRO * TILES, HALF, 2]),
+            )
+
+        def widen_on_gpsimd(c, h):
+            wide, raw = rotation_views(c, h)
+            nc.gpsimd.tensor_scalar(out=wide, in0=raw, scalar1=1.0, scalar2=0.0, op0=ALU.mult, op1=ALU.add)
+
+        def widen_on_scalar(c, h):
+            wide, raw = rotation_views(c, h)
+            nc.scalar.copy(out=wide, in_=raw)
+
+        w_grouped = const.tile([P, W_COLS, PACK], BF16, align_bytes=64)
+        w_codes = const.tile([P, W_COLS], U32, align_bytes=64)
+        w_scales = const.tile([P, W_COLS], U8, align_bytes=64)
+
+        def regroup_v_weight():
+            nc.gpsimd.tensor_scalar(
+                out=w_grouped[:, V_AT : V_AT + V_COLS, :],
+                in0=w_raw[2][:].rearrange("p j n -> p n j"),
                 scalar1=1.0,
                 scalar2=0.0,
                 op0=ALU.mult,
                 op1=ALU.add,
             )
 
-        w_grouped = const.tile([P, W_COLS, PACK], BF16, align_bytes=64)
-        w_codes = const.tile([P, W_COLS], U32, align_bytes=64)
-        w_scales = const.tile([P, W_COLS], U8, align_bytes=64)
-
-        def regroup_weights(o):
-            if o == 2:
-                nc.vector.tensor_copy(
-                    out=w_grouped[:, V_AT : V_AT + V_COLS, :], in_=w_raw[2][:].rearrange("p j n -> p n j")
-                )
-                return
+        def regroup_rope_weight(o):
             by_col = w_raw[o][:].rearrange("p j (h d) -> p h d j", h=H)
             head_cols = H * ROT
             plain_at = ROPE_AT + o * head_cols
-            nc.vector.tensor_copy(
+            nc.scalar.copy(
                 out=w_grouped[:, plain_at : plain_at + head_cols, :].rearrange("p (h f) j -> p h f j", h=H),
                 in_=by_col[:, :, 0:ROT, :],
             )
             swap_at = ROPE_AT + HEADS_QK * ROT + o * head_cols
             swapped = w_grouped[:, swap_at : swap_at + head_cols, :].rearrange("p (h a e) j -> p h a e j", h=H, e=2)
             pairs = by_col[:, :, 0:ROT, :].rearrange("p h (a e) j -> p h a e j", e=2)
-            nc.vector.tensor_scalar(
-                out=swapped[:, :, :, 0, :], in0=pairs[:, :, :, 1, :], scalar1=-1.0, scalar2=None, op0=ALU.mult
-            )
-            nc.vector.tensor_copy(out=swapped[:, :, :, 1, :], in_=pairs[:, :, :, 0, :])
+            nc.scalar.mul(out=swapped[:, :, :, 0, :], in_=pairs[:, :, :, 1, :], mul=-1.0)
+            nc.scalar.copy(out=swapped[:, :, :, 1, :], in_=pairs[:, :, :, 0, :])
+
+        def regroup_pass_weight(o):
+            by_col = w_raw[o][:].rearrange("p j (h d) -> p h d j", h=H)
             pass_cols = H * (DH - ROT)
             pass_at = PASS_AT + o * pass_cols
-            nc.vector.tensor_copy(
+            nc.scalar.copy(
                 out=w_grouped[:, pass_at : pass_at + pass_cols, :].rearrange("p (h d) j -> p h d j", h=H),
                 in_=by_col[:, :, ROT:DH, :],
             )
@@ -162,191 +182,230 @@ def tile_transformerlayershard_pa_t_kernel(
                     in_=w_grouped[:, lo:hi, :].rearrange("p c j -> p (c j)"),
                 )
 
-        def token_stats(m, i):
+        def token_stats(u, i):
+            n = UNITS[u][2]
             if i == 0:
-                stats_of[m] = small.tile([P, TILES, 6], F32, name="stats")
-            nc.vector.bn_stats(out=stats_of[m][:, i, :], in_=x_of[m][:, i, :])
+                stats_of[u] = small.tile([P, TILES, 6], F32, name="stats")
+            if i < n:
+                nc.vector.bn_stats(out=stats_of[u][:, i, :], in_=x_of[u][:, i, :])
 
-        def mean_and_variance(m):
-            mean_var_of[m] = small.tile([P, TILES, 2], F32, name="mean_var")
-            for i in range(TILES):
-                nc.vector.bn_aggr(out=mean_var_of[m][:, i, :], in_=stats_of[m][:, i, :])
+        def mean_and_variance(u):
+            mean_var_of[u] = small.tile([P, TILES, 2], F32, name="mean_var")
+            for i in range(UNITS[u][2]):
+                nc.vector.bn_aggr(out=mean_var_of[u][:, i, :], in_=stats_of[u][:, i, :])
 
-        def std_dev(m):
-            std_of[m] = small.tile([P, TILES], F32, name="std")
-            nc.scalar.activation(out=std_of[m][:], in_=mean_var_of[m][:, :, 1], func=ACT.Sqrt, bias=eps_col[:])
-
-        def negate_mean(m):
-            neg_mean_of[m] = small.tile([P, TILES], F32, name="neg_mean")
-            nc.gpsimd.tensor_scalar(
-                out=neg_mean_of[m][:], in0=mean_var_of[m][:, :, 0], scalar1=-1.0, scalar2=0.0, op0=ALU.mult, op1=ALU.add
+        def inverse_std(u):
+            n = UNITS[u][2]
+            rstd_of[u] = small.tile([P, TILES], F32, name="rstd")
+            nc.scalar.activation(
+                out=rstd_of[u][:, 0:n], in_=mean_var_of[u][:, 0:n, 1], func=ACT.Abs_reciprocal_sqrt, bias=eps_col[:]
             )
 
-        def inverse_std(m):
-            rstd_of[m] = small.tile([P, TILES], F32, name="rstd")
-            nc.vector.reciprocal(out=rstd_of[m][:], in_=std_of[m][:])
+        def negate_mean(u):
+            n = UNITS[u][2]
+            neg_mean_of[u] = small.tile([P, TILES], F32, name="neg_mean")
+            nc.scalar.mul(out=neg_mean_of[u][:, 0:n], in_=mean_var_of[u][:, 0:n, 0], mul=-1.0)
 
-        def normalise_on_gpsimd(m):
-            z_of[m] = z_pool.tile([P, TILES, PACK, P], F32, name="z")
-            shift_of[m] = small.tile([P, TILES - GPSIMD_TILES], F32, name="shift")
-            nc.gpsimd.tensor_tensor(
-                out=shift_of[m][:],
-                in0=neg_mean_of[m][:, GPSIMD_TILES:TILES],
-                in1=rstd_of[m][:, GPSIMD_TILES:TILES],
-                op=ALU.mult,
+        def tile_views(u, i):
+            if u not in z_of:
+                z_of[u] = z_pool.tile([P, TILES, PACK, P], F32, name="z")
+            return z_of[u][:, i, :, :], x_of[u][:, i, :].rearrange("p (c j) -> p j c", j=PACK)
+
+        def normalise(u, engine, i):
+            z, x_tile = tile_views(u, i)
+            engine.tensor_scalar(
+                out=z,
+                in0=x_tile,
+                scalar1=neg_mean_of[u][:, i : i + 1],
+                scalar2=rstd_of[u][:, i : i + 1],
+                op0=ALU.add,
+                op1=ALU.mult,
             )
-            for i in range(GPSIMD_TILES):
-                nc.gpsimd.tensor_scalar(
-                    out=z_of[m][:, i, :, :],
-                    in0=x_of[m][:, i, :].rearrange("p (c j) -> p j c", j=PACK),
-                    scalar1=neg_mean_of[m][:, i : i + 1],
-                    scalar2=rstd_of[m][:, i : i + 1],
-                    op0=ALU.add,
-                    op1=ALU.mult,
-                )
 
-        def normalise_on_scalar(m):
-            for i in range(GPSIMD_TILES, TILES):
-                nc.scalar.activation(
-                    out=z_of[m][:, i, :, :],
-                    in_=x_of[m][:, i, :].rearrange("p (c j) -> p j c", j=PACK),
-                    func=ACT.Identity,
-                    scale=rstd_of[m][:, i : i + 1],
-                    bias=shift_of[m][:, i - GPSIMD_TILES : i - GPSIMD_TILES + 1],
-                )
+        def normalise_on_gpsimd(u):
+            for i in range(UNITS[u][2] - 1):
+                normalise(u, nc.gpsimd, i)
 
-        def transpose(m):
-            planes_ps_of[m] = [bank("plane_ps%d" % j) for j in range(PACK)]
+        def normalise_last_tile(u):
+            i = UNITS[u][2] - 1
+            if u >= SCALAR_NORM_UNITS:
+                normalise(u, nc.vector, i)
+                return
+            z, x_tile = tile_views(u, i)
+            shift = small.tile([P, 1], F32, name="shift")
+            rstd = rstd_of[u][:, i : i + 1]
+            nc.scalar.activation(out=shift[:], in_=neg_mean_of[u][:, i : i + 1], func=ACT.Identity, scale=rstd)
+            nc.scalar.activation(out=z, in_=x_tile, func=ACT.Identity, scale=rstd, bias=shift[:])
+
+        def plane(u, j):
+            n = UNITS[u][2]
+            return j * n // TILES, j * n % TILES * P
+
+        def transpose(u):
+            n = UNITS[u][2]
+            planes_ps_of[u] = [bank("plane_ps%d" % b) for b in range(n)]
             for j in range(PACK):
-                for i in range(TILES):
+                b, at = plane(u, j)
+                for i in range(n):
                     nc.tensor.transpose(
-                        planes_ps_of[m][j][:, i * P : (i + 1) * P], z_of[m][:, i, j, :], ident[:]
+                        planes_ps_of[u][b][:, at + i * P : at + (i + 1) * P], z_of[u][:, i, j, :], ident[:]
                     )
 
-        def scale_shift(m):
-            planes_of[m] = work.tile([P, PACK, MACRO], BF16, name="xn_planes")
-            for j in range(PACK):
-                nc.scalar.activation(
-                    out=planes_of[m][:, j, :],
-                    in_=planes_ps_of[m][j][:],
-                    func=ACT.Identity,
-                    scale=affine[:, j : j + 1],
-                    bias=affine[:, PACK + j : PACK + j + 1],
-                )
+        def scale_shift(u, j):
+            n = UNITS[u][2]
+            if j == 0:
+                planes_of[u] = work.tile([P, PACK, MACRO], BF16, name="xn_planes")
+            b, at = plane(u, j)
+            nc.scalar.activation(
+                out=planes_of[u][:, j, 0 : n * P],
+                in_=planes_ps_of[u][b][:, at : at + n * P],
+                func=ACT.Identity,
+                scale=affine[:, j : j + 1],
+                bias=affine[:, PACK + j : PACK + j + 1],
+            )
 
-        def regroup(m):
-            grouped_of[m] = work.tile([P, MACRO, PACK], BF16, align_bytes=64, name="xn_grouped")
+        def regroup(u):
+            cols = UNITS[u][2] * P
+            grouped_of[u] = work.tile([P, MACRO, PACK], BF16, align_bytes=64, name="xn_grouped")
             nc.vector.tensor_copy(
-                out=grouped_of[m][:].rearrange("p (c r) j -> p c j r", r=4),
-                in_=planes_of[m][:].rearrange("p j (c r) -> p c j r", r=4),
+                out=grouped_of[u][:, 0:cols, :].rearrange("p (c r) j -> p c j r", r=4),
+                in_=planes_of[u][:, :, 0:cols].rearrange("p j (c r) -> p c j r", r=4),
             )
 
-        def quantise(m):
-            codes_of[m] = work.tile([P, MACRO], U32, align_bytes=64, name="xn_codes")
-            scales_of[m] = work.tile([P, MACRO], U8, align_bytes=64, name="xn_scales")
+        def quantise(u):
+            cols = UNITS[u][2] * P
+            codes_of[u] = work.tile([P, MACRO], U32, align_bytes=64, name="xn_codes")
+            scales_of[u] = work.tile([P, MACRO], U8, align_bytes=64, name="xn_scales")
             nc.vector.quantize_mx(
-                out=codes_of[m][:].bitcast(FP8X4),
-                scales=scales_of[m][:],
-                in_=grouped_of[m][:].rearrange("p t j -> p (t j)"),
+                out=codes_of[u][:, 0:cols].bitcast(FP8X4),
+                scales=scales_of[u][:, 0:cols],
+                in_=grouped_of[u][:, 0:cols, :].rearrange("p t j -> p (t j)"),
             )
 
-        def one_pass(m, i, out_ps, at, cols):
+        def one_pass(u, i, out_ps, at, cols):
             nc.tensor.matmul_mx(
                 out=out_ps,
-                lhsT=codes_of[m][:, i * P : (i + 1) * P].bitcast(FP8X4),
-                lhsT_scale=scales_of[m][:, i * P : (i + 1) * P],
+                lhsT=codes_of[u][:, i * P : (i + 1) * P].bitcast(FP8X4),
+                lhsT_scale=scales_of[u][:, i * P : (i + 1) * P],
                 rhs=w_codes[:, at : at + cols].bitcast(FP8X4),
                 rhs_scale=w_scales[:, at : at + cols],
                 start=True,
                 stop=True,
             )
 
-        def project(m, pair):
-            first = 2 * pair
+        def pair_tiles(u, pair):
+            return range(2 * pair, min(2 * pair + 2, UNITS[u][2]))
+
+        def project(u, pair):
+            tiles = pair_tiles(u, pair)
+            if not tiles:
+                return
             rope_ps = bank("rope_ps")
             v_ps = bank("v_ps")
-            pass_ps = [bank("pass_ps%d" % n) for n in range(2)]
-            banks_of[(m, pair)] = (v_ps, pass_ps, rope_ps)
-            for n in range(2):
-                one_pass(m, first + n, rope_ps[:, n * ROPE_COLS : (n + 1) * ROPE_COLS], ROPE_AT, ROPE_COLS)
-            for n in range(2):
-                one_pass(m, first + n, v_ps[:, n * V_COLS : (n + 1) * V_COLS], V_AT, V_COLS)
-            for n in range(2):
-                one_pass(m, first + n, pass_ps[n][:, 0:256], PASS_AT, 256)
-                one_pass(m, first + n, pass_ps[n][:, 256:PASS_COLS], PASS_AT + 256, PASS_COLS - 256)
+            pass_ps = [bank("pass_ps%d" % n) for n in range(len(tiles))]
+            banks_of[(u, pair)] = (v_ps, pass_ps, rope_ps)
+            for n, i in enumerate(tiles):
+                one_pass(u, i, rope_ps[:, n * ROPE_COLS : (n + 1) * ROPE_COLS], ROPE_AT, ROPE_COLS)
+            for n, i in enumerate(tiles):
+                one_pass(u, i, v_ps[:, n * V_COLS : (n + 1) * V_COLS], V_AT, V_COLS)
+            for n, i in enumerate(tiles):
+                one_pass(u, i, pass_ps[n][:, 0:256], PASS_AT, 256)
+                one_pass(u, i, pass_ps[n][:, 256:PASS_COLS], PASS_AT + 256, PASS_COLS - 256)
 
-        def copy_out(m, pair):
-            first = 2 * pair
+        def copy_out(u, pair):
+            tiles = pair_tiles(u, pair)
             if pair == 0:
-                stage_of[m] = out_pool.tile([P, 3, TILES, E], F32, name="stage")
-            stage = stage_of[m]
-            v_ps, pass_ps, rope_ps = banks_of[(m, pair)]
-            nc.scalar.copy(out=stage[:, 2, first : first + 2, :].rearrange("p i c -> p (i c)"), in_=v_ps[:])
-            for n in range(2):
+                stage_of[u] = out_pool.tile([P, 3, UNITS[u][2], E], F32, name="stage%d" % UNITS[u][2])
+            if not tiles:
+                return
+            stage = stage_of[u]
+            v_ps, pass_ps, rope_ps = banks_of[(u, pair)]
+            v_out = stage[:, 2, tiles.start : tiles.stop, :].rearrange("p i c -> p (i c)")
+            v_in = v_ps[:, 0 : len(tiles) * V_COLS]
+            if u < VECTOR_COPY_FROM:
+                nc.scalar.copy(out=v_out, in_=v_in)
+            else:
+                nc.vector.tensor_copy(out=v_out, in_=v_in)
+            for n, i in enumerate(tiles):
                 nc.scalar.copy(
-                    out=stage[:, 0:2, first + n, :].rearrange("p o (h d) -> p o h d", h=H)[:, :, :, ROT:DH],
+                    out=stage[:, 0:2, i, :].rearrange("p o (h d) -> p o h d", h=H)[:, :, :, ROT:DH],
                     in_=pass_ps[n][:, 0:PASS_COLS].rearrange("p (o h d) -> p o h d", o=2, h=H),
                 )
 
-        def rope_products(m, pair):
-            first = 2 * pair
+        def rope_products(u, pair):
+            m, i0, n = UNITS[u]
+            tiles = pair_tiles(u, pair)
             if pair == 0:
-                products_of[m] = out_pool.tile([P, TILES, 2, HEADS_QK, ROT], F32, name="products")
-            v_ps, pass_ps, rope_ps = banks_of[(m, pair)]
-            pos = (m % POS_MACRO) * TILES + first
+                products_of[u] = out_pool.tile([P, 2, n, 2, H * ROT], F32, name="products%d" % n)
+            if not tiles:
+                return
+            v_ps, pass_ps, rope_ps = banks_of[(u, pair)]
+            pos = (m % POS_MACRO) * TILES + i0 + tiles.start
             nc.vector.tensor_tensor(
-                out=products_of[m][:, first : first + 2, :, :, :].rearrange("p i c g f -> p (i c) g f"),
-                in0=rope_ps[:].rearrange("p (a g f) -> p a g f", g=HEADS_QK, f=ROT),
-                in1=rot[:, pos : pos + 2, :, :]
-                .rearrange("p i c f -> p (i c) f")
+                out=products_of[u][:, :, tiles.start : tiles.stop, :, :].rearrange("p o i c y -> p (i c) o y"),
+                in0=rope_ps[:, 0 : len(tiles) * ROPE_COLS].rearrange("p (a o y) -> p a o y", o=2, y=H * ROT),
+                in1=rot[:, pos : pos + len(tiles), :, :, :]
+                .rearrange("p i c h f -> p (i c) (h f)")
                 .unsqueeze(2)
-                .to_broadcast([P, 4, HEADS_QK, ROT]),
+                .to_broadcast([P, 2 * len(tiles), 2, H * ROT]),
                 op=ALU.mult,
             )
 
-        def store(m, o):
-            nc.sync.dma_start(out=out_rows[o][m], in_=stage_of[m][:, o, :, :].rearrange("p i c -> p (i c)"))
+        def store(u, o):
+            m, i0, n = UNITS[u]
+            nc.sync.dma_start(
+                out=out_rows[o][m][:, i0 * E : (i0 + n) * E], in_=stage_of[u][:, o, :, :].rearrange("p i c -> p (i c)")
+            )
 
-        def rotate_and_store(m):
-            for o in range(2):
-                nc.gpsimd.tensor_tensor(
-                    out=stage_of[m][:, o, :, :].rearrange("p i (h d) -> p i h d", h=H)[:, :, :, 0:ROT],
-                    in0=products_of[m][:, :, 0, o * H : (o + 1) * H, :],
-                    in1=products_of[m][:, :, 1, o * H : (o + 1) * H, :],
-                    op=ALU.add,
-                )
-                store(m, o)
+        def rotate(u):
+            nc.gpsimd.tensor_tensor(
+                out=stage_of[u][:, 0:2, :, :].rearrange("p o i (h d) -> p (o i) h d", h=H)[:, :, :, 0:ROT],
+                in0=products_of[u][:, :, :, 0, :].rearrange("p o i (h f) -> p (o i) h f", h=H),
+                in1=products_of[u][:, :, :, 1, :].rearrange("p o i (h f) -> p (o i) h f", h=H),
+                op=ALU.add,
+            )
 
-        def when(m, stage, *args):
-            if 0 <= m < N_MACRO:
-                stage(m, *args)
+        def when(u, stage, *args):
+            if 0 <= u < len(UNITS):
+                stage(u, *args)
 
-        for s in range(-LOAD_AHEAD, N_MACRO + 1):
-            if s + LOAD_AHEAD > 0:
-                when(s + LOAD_AHEAD, load)
-            when(s + NORM_AHEAD, std_dev)
+        for s in range(-STATS_AHEAD, len(UNITS)):
+            when(s, quantise)
+            when(s + TRANSPOSE_AHEAD, normalise_last_tile)
+            when(s + GROUP_AHEAD, regroup)
+            for j in range(PACK - 1):
+                when(s + PLANES_AHEAD, scale_shift, j)
             when(s + NORM_AHEAD, negate_mean)
-            when(s - 1, rotate_and_store)
-            when(s + QUANT_AHEAD, regroup)
+            when(s + NORM_AHEAD, inverse_std)
+            when(s + PLANES_AHEAD, scale_shift, PACK - 1)
+            when(s, project, 0)
             when(s, rope_products, 0)
             when(s, copy_out, 0)
-            when(s, project, 1)
-            when(s + QUANT_AHEAD, quantise)
-            when(s + NORM_AHEAD, inverse_std)
             when(s + NORM_AHEAD, normalise_on_gpsimd)
             when(s + STATS_AHEAD, token_stats, 0)
             when(s + STATS_AHEAD, token_stats, 1)
-            when(s + PLANES_AHEAD, scale_shift)
-            when(s + QUANT_AHEAD, project, 0)
-            when(s + STATS_AHEAD, token_stats, 2)
-            when(s + NORM_AHEAD, normalise_on_scalar)
+            when(s, project, 1)
             when(s, rope_products, 1)
             when(s, copy_out, 1)
             when(s, store, 2)
-            when(s + NORM_AHEAD, transpose)
+            when(s, rotate)
+            when(s, store, 0)
+            when(s, store, 1)
+            when(s + TRANSPOSE_AHEAD, transpose)
+            when(s + STATS_AHEAD, token_stats, 2)
             when(s + STATS_AHEAD, token_stats, 3)
             when(s + STATS_AHEAD, mean_and_variance)
-            if 0 <= s + STATS_AHEAD < 3:
-                regroup_weights(s + STATS_AHEAD)
-            if s + PLANES_AHEAD == 0:
+            if s == -STATS_AHEAD:
+                regroup_v_weight()
+                regroup_rope_weight(0)
+                widen_on_gpsimd(0, 0)
+            elif s == 1 - STATS_AHEAD:
+                regroup_rope_weight(1)
+                widen_on_gpsimd(1, 0)
+            elif s == 2 - STATS_AHEAD:
+                regroup_pass_weight(0)
+                widen_on_scalar(0, 1)
+            elif s == 3 - STATS_AHEAD:
+                regroup_pass_weight(1)
                 quantise_weights()
+                widen_on_scalar(1, 1)

@@ -42,11 +42,12 @@ UNITS = (
     + [(N_MACRO - 1, 0, 2), (N_MACRO - 1, 2, 1), (N_MACRO - 1, 3, 1)]
 )
 
-STATS_AHEAD = 5
-NORM_AHEAD = 4
-TRANSPOSE_AHEAD = 3
-PLANES_AHEAD = 2
-GROUP_AHEAD = 1
+STATS_AHEAD = 6
+NORM_AHEAD = 5
+TRANSPOSE_AHEAD = 4
+PLANES_AHEAD = 3
+GROUP_AHEAD = 2
+QUANT_AHEAD = 1
 
 SCALAR_NORM_UNITS = 9
 VECTOR_COPY_FROM = len(UNITS) - 5
@@ -370,7 +371,7 @@ def tile_transformerlayershard_pa_t_kernel(
                 stage(u, *args)
 
         for s in range(-STATS_AHEAD, len(UNITS)):
-            when(s, quantise)
+            when(s + QUANT_AHEAD, quantise)
             when(s + TRANSPOSE_AHEAD, normalise_last_tile)
             when(s + GROUP_AHEAD, regroup)
             for j in range(PACK - 1):

@@ -36,21 +36,25 @@ W_COLS = PASS_AT + PASS_COLS
 
 FLOPS = 2 * TOKENS * D * 3 * E
 
-UNITS = (
-    [(0, 0, 1), (0, 1, 1), (0, 2, 2)]
-    + [(m, 0, TILES) for m in range(1, N_MACRO - 1)]
-    + [(N_MACRO - 1, 0, 2), (N_MACRO - 1, 2, 1), (N_MACRO - 1, 3, 1)]
-)
+HEAD = (2, 2)
+TAIL = (2, 2)
+SIZES = HEAD + (TILES,) * (N_MACRO - (sum(HEAD) + sum(TAIL)) // TILES) + TAIL
+STARTS = [sum(SIZES[:u]) for u in range(len(SIZES))]
+UNITS = [(STARTS[u] // TILES, STARTS[u] % TILES, SIZES[u]) for u in range(len(SIZES))]
 
-STATS_AHEAD = 6
-NORM_AHEAD = 5
-TRANSPOSE_AHEAD = 4
-PLANES_AHEAD = 3
-GROUP_AHEAD = 2
-QUANT_AHEAD = 1
+STATS_AHEAD = 3
+GPSIMD_AHEAD = 2
+PLANES_AHEAD = 1
 
-SCALAR_NORM_UNITS = 9
-VECTOR_COPY_FROM = len(UNITS) - 5
+SHARE = 0
+V_HEAD = 1
+WK_PASS = 1
+WK_ROPE = 1
+RSTD_AT = 1
+SCALAR_NORM_AT = 3
+LOAD_FIRST = 2
+LOAD_AHEAD = 8
+VECTOR_COPY_FROM = len(UNITS) - 1
 
 
 def tile_transformerlayershard_pa_t_kernel(
@@ -84,8 +88,8 @@ def tile_transformerlayershard_pa_t_kernel(
             x_of[u] = const.tile([P, n, D], BF16, name="x_sb%d" % u)
             nc.sync.dma_start(out=x_of[u][:].rearrange("p i k -> p (i k)"), in_=x_rows[m][:, i0 * D : (i0 + n) * D])
 
-        load(0)
-        load(1)
+        for u in range(LOAD_FIRST):
+            load(u)
 
         affine_raw = []
         for c, vec in enumerate((ln_scale, ln_offset)):
@@ -102,7 +106,7 @@ def tile_transformerlayershard_pa_t_kernel(
             raw = const.tile([P, POS_MACRO, TILES * HALF], BF16, name="rot_raw%d" % c)
             nc.scalar.dma_start(out=raw[:], in_=table.rearrange("(m p i) a -> p m (i a)", p=P, i=TILES))
             rot_raw.append(raw)
-        for u in range(2, len(UNITS)):
+        for u in range(LOAD_FIRST, LOAD_AHEAD - STATS_AHEAD):
             load(u)
 
         one_col = const.tile([P, 1], F32)
@@ -121,21 +125,25 @@ def tile_transformerlayershard_pa_t_kernel(
 
         rot = const.tile([P, POS_MACRO * TILES, 2, H, ROT], F32)
 
-        def rotation_views(c, h):
+        HALF_POS = POS_MACRO // 2
+
+        def rotation_views(c, h, half):
+            tiles = slice(half * HALF_POS * TILES, (half + 1) * HALF_POS * TILES)
+            macros = slice(half * HALF_POS, (half + 1) * HALF_POS)
             return (
-                rot[:, :, c, h, :].rearrange("p t (a e) -> p t a e", e=2),
-                rot_raw[c][:]
+                rot[:, tiles, c, h, :].rearrange("p t (a e) -> p t a e", e=2),
+                rot_raw[c][:, macros, :]
                 .rearrange("p m (i a) -> p (m i) a", a=HALF)
                 .unsqueeze(3)
-                .to_broadcast([P, POS_MACRO * TILES, HALF, 2]),
+                .to_broadcast([P, HALF_POS * TILES, HALF, 2]),
             )
 
-        def widen_on_gpsimd(c, h):
-            wide, raw = rotation_views(c, h)
+        def widen_on_gpsimd(c, h, half):
+            wide, raw = rotation_views(c, h, half)
             nc.gpsimd.tensor_scalar(out=wide, in0=raw, scalar1=1.0, scalar2=0.0, op0=ALU.mult, op1=ALU.add)
 
-        def widen_on_scalar(c, h):
-            wide, raw = rotation_views(c, h)
+        def widen_on_scalar(c, h, half):
+            wide, raw = rotation_views(c, h, half)
             nc.scalar.copy(out=wide, in_=raw)
 
         w_grouped = const.tile([P, W_COLS, PACK], BF16, align_bytes=64)
@@ -152,27 +160,40 @@ def tile_transformerlayershard_pa_t_kernel(
                 op1=ALU.add,
             )
 
-        def regroup_rope_weight(o):
+        def moved(engine, out, in_):
+            if engine is nc.scalar:
+                nc.scalar.copy(out=out, in_=in_)
+            else:
+                engine.tensor_copy(out=out, in_=in_)
+
+        def regroup_rope_weight(engine, o):
             by_col = w_raw[o][:].rearrange("p j (h d) -> p h d j", h=H)
             head_cols = H * ROT
             plain_at = ROPE_AT + o * head_cols
-            nc.scalar.copy(
-                out=w_grouped[:, plain_at : plain_at + head_cols, :].rearrange("p (h f) j -> p h f j", h=H),
-                in_=by_col[:, :, 0:ROT, :],
+            moved(
+                engine,
+                w_grouped[:, plain_at : plain_at + head_cols, :].rearrange("p (h f) j -> p h f j", h=H),
+                by_col[:, :, 0:ROT, :],
             )
             swap_at = ROPE_AT + HEADS_QK * ROT + o * head_cols
             swapped = w_grouped[:, swap_at : swap_at + head_cols, :].rearrange("p (h a e) j -> p h a e j", h=H, e=2)
             pairs = by_col[:, :, 0:ROT, :].rearrange("p h (a e) j -> p h a e j", e=2)
-            nc.scalar.mul(out=swapped[:, :, :, 0, :], in_=pairs[:, :, :, 1, :], mul=-1.0)
-            nc.scalar.copy(out=swapped[:, :, :, 1, :], in_=pairs[:, :, :, 0, :])
+            if engine is nc.scalar:
+                nc.scalar.mul(out=swapped[:, :, :, 0, :], in_=pairs[:, :, :, 1, :], mul=-1.0)
+            else:
+                engine.tensor_scalar(
+                    out=swapped[:, :, :, 0, :], in0=pairs[:, :, :, 1, :], scalar1=-1.0, scalar2=None, op0=ALU.mult
+                )
+            moved(engine, swapped[:, :, :, 1, :], pairs[:, :, :, 0, :])
 
-        def regroup_pass_weight(o):
+        def regroup_pass_weight(engine, o):
             by_col = w_raw[o][:].rearrange("p j (h d) -> p h d j", h=H)
             pass_cols = H * (DH - ROT)
             pass_at = PASS_AT + o * pass_cols
-            nc.scalar.copy(
-                out=w_grouped[:, pass_at : pass_at + pass_cols, :].rearrange("p (h d) j -> p h d j", h=H),
-                in_=by_col[:, :, ROT:DH, :],
+            moved(
+                engine,
+                w_grouped[:, pass_at : pass_at + pass_cols, :].rearrange("p (h d) j -> p h d j", h=H),
+                by_col[:, :, ROT:DH, :],
             )
 
         def quantise_weights():
@@ -203,6 +224,8 @@ def tile_transformerlayershard_pa_t_kernel(
             )
 
         def negate_mean(u):
+            if u in neg_mean_of:
+                return
             n = UNITS[u][2]
             neg_mean_of[u] = small.tile([P, TILES], F32, name="neg_mean")
             nc.scalar.mul(out=neg_mean_of[u][:, 0:n], in_=mean_var_of[u][:, 0:n, 0], mul=-1.0)
@@ -212,31 +235,44 @@ def tile_transformerlayershard_pa_t_kernel(
                 z_of[u] = z_pool.tile([P, TILES, PACK, P], F32, name="z")
             return z_of[u][:, i, :, :], x_of[u][:, i, :].rearrange("p (c j) -> p j c", j=PACK)
 
-        def normalise(u, engine, i):
-            z, x_tile = tile_views(u, i)
-            engine.tensor_scalar(
-                out=z,
-                in0=x_tile,
-                scalar1=neg_mean_of[u][:, i : i + 1],
-                scalar2=rstd_of[u][:, i : i + 1],
-                op0=ALU.add,
-                op1=ALU.mult,
-            )
-
         def normalise_on_gpsimd(u):
-            for i in range(UNITS[u][2] - 1):
-                normalise(u, nc.gpsimd, i)
+            for i in range(0 if u < V_HEAD else UNITS[u][2] - 1):
+                z, x_tile = tile_views(u, i)
+                nc.gpsimd.tensor_scalar(
+                    out=z,
+                    in0=x_tile,
+                    scalar1=neg_mean_of[u][:, i : i + 1],
+                    scalar2=rstd_of[u][:, i : i + 1],
+                    op0=ALU.add,
+                    op1=ALU.mult,
+                )
 
-        def normalise_last_tile(u):
-            i = UNITS[u][2] - 1
-            if u >= SCALAR_NORM_UNITS:
-                normalise(u, nc.vector, i)
+        def normalise_on_vector(u):
+            n = UNITS[u][2]
+            head = u < V_HEAD
+            for i in range(0 if head else n - 1, n):
+                z, x_tile = tile_views(u, i)
+                lo = 0 if head else SHARE
+                nc.vector.tensor_scalar(
+                    out=z[:, lo:, :],
+                    in0=x_tile[:, lo:, :],
+                    scalar1=mean_var_of[u][:, i, 0:1],
+                    scalar2=rstd_of[u][:, i : i + 1],
+                    op0=ALU.subtract,
+                    op1=ALU.mult,
+                )
+
+        def normalise_on_scalar(u):
+            if u < V_HEAD or SHARE == 0:
                 return
+            i = UNITS[u][2] - 1
             z, x_tile = tile_views(u, i)
             shift = small.tile([P, 1], F32, name="shift")
             rstd = rstd_of[u][:, i : i + 1]
             nc.scalar.activation(out=shift[:], in_=neg_mean_of[u][:, i : i + 1], func=ACT.Identity, scale=rstd)
-            nc.scalar.activation(out=z, in_=x_tile, func=ACT.Identity, scale=rstd, bias=shift[:])
+            nc.scalar.activation(
+                out=z[:, 0:SHARE, :], in_=x_tile[:, 0:SHARE, :], func=ACT.Identity, scale=rstd, bias=shift[:]
+            )
 
         def plane(u, j):
             n = UNITS[u][2]
@@ -313,24 +349,24 @@ def tile_transformerlayershard_pa_t_kernel(
                 one_pass(u, i, pass_ps[n][:, 0:256], PASS_AT, 256)
                 one_pass(u, i, pass_ps[n][:, 256:PASS_COLS], PASS_AT + 256, PASS_COLS - 256)
 
-        def copy_out(u, pair):
+        def copy_v(u, pair):
             tiles = pair_tiles(u, pair)
             if pair == 0:
                 stage_of[u] = out_pool.tile([P, 3, UNITS[u][2], E], F32, name="stage%d" % UNITS[u][2])
             if not tiles:
                 return
-            stage = stage_of[u]
-            v_ps, pass_ps, rope_ps = banks_of[(u, pair)]
-            v_out = stage[:, 2, tiles.start : tiles.stop, :].rearrange("p i c -> p (i c)")
-            v_in = v_ps[:, 0 : len(tiles) * V_COLS]
+            v_out = stage_of[u][:, 2, tiles.start : tiles.stop, :].rearrange("p i c -> p (i c)")
+            v_in = banks_of[(u, pair)][0][:, 0 : len(tiles) * V_COLS]
             if u < VECTOR_COPY_FROM:
                 nc.scalar.copy(out=v_out, in_=v_in)
             else:
                 nc.vector.tensor_copy(out=v_out, in_=v_in)
-            for n, i in enumerate(tiles):
+
+        def copy_pass(u, pair):
+            for n, i in enumerate(pair_tiles(u, pair)):
                 nc.scalar.copy(
-                    out=stage[:, 0:2, i, :].rearrange("p o (h d) -> p o h d", h=H)[:, :, :, ROT:DH],
-                    in_=pass_ps[n][:, 0:PASS_COLS].rearrange("p (o h d) -> p o h d", o=2, h=H),
+                    out=stage_of[u][:, 0:2, i, :].rearrange("p o (h d) -> p o h d", h=H)[:, :, :, ROT:DH],
+                    in_=banks_of[(u, pair)][1][n][:, 0:PASS_COLS].rearrange("p (o h d) -> p o h d", o=2, h=H),
                 )
 
         def rope_products(u, pair):
@@ -370,43 +406,58 @@ def tile_transformerlayershard_pa_t_kernel(
             if 0 <= u < len(UNITS):
                 stage(u, *args)
 
-        for s in range(-STATS_AHEAD, len(UNITS)):
-            when(s + QUANT_AHEAD, quantise)
-            when(s + TRANSPOSE_AHEAD, normalise_last_tile)
-            when(s + GROUP_AHEAD, regroup)
-            for j in range(PACK - 1):
-                when(s + PLANES_AHEAD, scale_shift, j)
-            when(s + NORM_AHEAD, negate_mean)
-            when(s + NORM_AHEAD, inverse_std)
-            when(s + PLANES_AHEAD, scale_shift, PACK - 1)
-            when(s, project, 0)
-            when(s, rope_products, 0)
-            when(s, copy_out, 0)
-            when(s + NORM_AHEAD, normalise_on_gpsimd)
+        for s in range(-STATS_AHEAD, len(UNITS) + 1):
+            if s + LOAD_AHEAD >= LOAD_AHEAD - STATS_AHEAD:
+                when(s + LOAD_AHEAD, load)
+            when(s - 1, rope_products, 1)
             when(s + STATS_AHEAD, token_stats, 0)
             when(s + STATS_AHEAD, token_stats, 1)
+            for j in range(PACK):
+                when(s + PLANES_AHEAD, scale_shift, j)
+            when(s + GPSIMD_AHEAD, normalise_on_gpsimd)
+            when(s - 1, rotate)
+            when(s - 1, store, 0)
+            when(s - 1, store, 1)
+            when(s, project, 0)
+            when(s, rope_products, 0)
+            when(s, copy_v, 0)
+            when(s, copy_pass, 0)
             when(s, project, 1)
-            when(s, rope_products, 1)
-            when(s, copy_out, 1)
-            when(s, store, 2)
-            when(s, rotate)
-            when(s, store, 0)
-            when(s, store, 1)
-            when(s + TRANSPOSE_AHEAD, transpose)
             when(s + STATS_AHEAD, token_stats, 2)
             when(s + STATS_AHEAD, token_stats, 3)
             when(s + STATS_AHEAD, mean_and_variance)
-            if s == -STATS_AHEAD:
+            if RSTD_AT == 0:
+                when(s + STATS_AHEAD, inverse_std)
+            if RSTD_AT == 1:
+                when(s, copy_v, 1)
+                when(s + STATS_AHEAD, inverse_std)
+            if RSTD_AT == 2:
+                when(s, copy_v, 1)
+                when(s, copy_pass, 1)
+                when(s + STATS_AHEAD, inverse_std)
+            when(s + PLANES_AHEAD, regroup)
+            when(s + STATS_AHEAD, normalise_on_vector)
+            when(s + PLANES_AHEAD, quantise)
+            if RSTD_AT < 1:
+                when(s, copy_v, 1)
+            if RSTD_AT < 2:
+                when(s, copy_pass, 1)
+            when(s, store, 2)
+            if s + STATS_AHEAD >= V_HEAD:
+                when(s + STATS_AHEAD, negate_mean)
+            when(s + STATS_AHEAD, normalise_on_scalar)
+            when(s + GPSIMD_AHEAD, transpose)
+            if s == -3:
                 regroup_v_weight()
-                regroup_rope_weight(0)
-                widen_on_gpsimd(0, 0)
-            elif s == 1 - STATS_AHEAD:
-                regroup_rope_weight(1)
-                widen_on_gpsimd(1, 0)
-            elif s == 2 - STATS_AHEAD:
-                regroup_pass_weight(0)
-                widen_on_scalar(0, 1)
-            elif s == 3 - STATS_AHEAD:
-                regroup_pass_weight(1)
+                regroup_rope_weight(nc.scalar, 0)
+                regroup_rope_weight(nc.scalar if WK_ROPE else nc.vector, 1)
+                regroup_pass_weight(nc.scalar if WK_PASS else nc.vector, 1)
+                widen_on_gpsimd(0, 0, 0)
+                widen_on_gpsimd(1, 0, 0)
+            elif s == -2:
+                regroup_pass_weight(nc.scalar, 0)
                 quantise_weights()
-                widen_on_scalar(1, 1)
+                widen_on_scalar(0, 1, 0)
+                widen_on_scalar(1, 1, 0)
+            elif 1 <= s <= 4:
+                widen_on_scalar((s - 1) // 2, (s - 1) % 2, 1)

@@ -73,7 +73,8 @@ def tile_transformerlayershard_pa_t_kernel(
         z_pool = ctx.enter_context(tc.tile_pool(name="z", bufs=3))
         work = ctx.enter_context(tc.tile_pool(name="work", bufs=2))
         out_pool = ctx.enter_context(tc.tile_pool(name="out", bufs=3))
-        psum = ctx.enter_context(tc.psum_pool(name="psum", bufs=BANKS))
+        psum = ctx.enter_context(tc.psum_pool(name="psum", bufs=BANKS - 2))
+        psum_rope = ctx.enter_context(tc.psum_pool(name="psum_rope", bufs=2))
         ctx.enter_context(tc.manual_schedule())
 
         def bank(name):
@@ -337,7 +338,7 @@ def tile_transformerlayershard_pa_t_kernel(
             tiles = pair_tiles(u, pair)
             if not tiles:
                 return
-            rope_ps = bank("rope_ps")
+            rope_ps = psum_rope.tile([P, BANK], F32, tag="rope", name="rope_ps")
             v_ps = bank("v_ps")
             pass_ps = [bank("pass_ps%d" % n) for n in range(len(tiles))]
             banks_of[(u, pair)] = (v_ps, pass_ps, rope_ps)

@@ -306,8 +306,8 @@ def tile_transformerlayershard_pa_t_kernel(
             cols = UNITS[u][2] * P
             grouped_of[u] = work.tile([P, MACRO, PACK], BF16, align_bytes=64, name="xn_grouped")
             nc.vector.tensor_copy(
-                out=grouped_of[u][:, 0:cols, :].rearrange("p (c r) j -> p c j r", r=4),
-                in_=planes_of[u][:, :, 0:cols].rearrange("p j (c r) -> p c j r", r=4),
+                out=grouped_of[u][:, 0:cols, :].rearrange("p (c r) j -> p c j r", r=8),
+                in_=planes_of[u][:, :, 0:cols].rearrange("p j (c r) -> p c j r", r=8),
             )
 
         def quantise(u):

from contextlib import ExitStack

import concourse.mybir as mybir
from concourse.masks import make_identity

F32 = mybir.dt.float32
BF16 = mybir.dt.bfloat16
U32 = mybir.dt.uint32
U8 = mybir.dt.uint8
FP8X4 = mybir.dt.float8_e4m3fn_x4
ALU = mybir.AluOpType
ACT = mybir.ActivationFunctionType

P = 128
PACK = 4
BANK = 512
BANKS = 8
B, T, D, H, DH, ROT = 2, 4096, 512, 2, 128, 32
E = H * DH
EPS = 1e-5
TOKENS = B * T
TILES = 4
MACRO = P * TILES
N_MACRO = TOKENS // MACRO
POS_MACRO = T // MACRO
HALF = ROT // 2
HEADS_QK = 2 * H

ROPE_COLS = 2 * HEADS_QK * ROT
V_COLS = E
PASS_COLS = HEADS_QK * (DH - ROT)
ROPE_AT = 0
V_AT = ROPE_AT + ROPE_COLS
PASS_AT = V_AT + V_COLS
W_COLS = PASS_AT + PASS_COLS

FLOPS = 2 * TOKENS * D * 3 * E

HEAD = (2, 2)
TAIL = (2, 2)
SIZES = HEAD + (TILES,) * (N_MACRO - (sum(HEAD) + sum(TAIL)) // TILES) + TAIL
STARTS = [sum(SIZES[:u]) for u in range(len(SIZES))]
UNITS = [(STARTS[u] // TILES, STARTS[u] % TILES, SIZES[u]) for u in range(len(SIZES))]

STATS_AHEAD = 3
GPSIMD_AHEAD = 2
PLANES_AHEAD = 1

SHARE = 0
V_HEAD = 1
WK_PASS = 1
WK_ROPE = 1
RSTD_AT = 1
SCALAR_NORM_AT = 3
LOAD_FIRST = 2
LOAD_AHEAD = 8
VECTOR_COPY_FROM = len(UNITS) - 1


def tile_transformerlayershard_pa_t_kernel(
    tc, x, ln_scale, ln_offset, wq, wk, wv, rope_cos, rope_sin, out_0, out_1, out_2
):
    nc = tc.nc
    x_rows = x.rearrange("b t k -> (b t) k").rearrange("(m p i) k -> m p (i k)", p=P, i=TILES)
    out_rows = [
        o.rearrange("b t h d -> (b t) (h d)").rearrange("(m p i) c -> m p (i c)", p=P, i=TILES)
        for o in (out_0, out_1, out_2)
    ]

    with ExitStack() as ctx:
        const = ctx.enter_context(tc.tile_pool(name="const", bufs=1))
        small = ctx.enter_context(tc.tile_pool(name="small", bufs=4))
        z_pool = ctx.enter_context(tc.tile_pool(name="z", bufs=3))
        work = ctx.enter_context(tc.tile_pool(name="work", bufs=2))
        out_pool = ctx.enter_context(tc.tile_pool(name="out", bufs=3))
        psum = ctx.enter_context(tc.psum_pool(name="psum", bufs=BANKS - 2))
        psum_rope = ctx.enter_context(tc.psum_pool(name="psum_rope", bufs=2))
        ctx.enter_context(tc.manual_schedule())

        def bank(name):
            return psum.tile([P, BANK], F32, tag="bank", name=name)

        x_of, stats_of, mean_var_of, rstd_of, neg_mean_of = {}, {}, {}, {}, {}
        z_of, planes_ps_of, planes_of, grouped_of, codes_of, scales_of = {}, {}, {}, {}, {}, {}
        banks_of, stage_of, products_of = {}, {}, {}

        def load(u):
            m, i0, n = UNITS[u]
            x_of[u] = const.tile([P, n, D], BF16, name="x_sb%d" % u)
            nc.sync.dma_start(out=x_of[u][:].rearrange("p i k -> p (i k)"), in_=x_rows[m][:, i0 * D : (i0 + n) * D])

        for u in range(LOAD_FIRST):
            load(u)

        affine_raw = []
        for c, vec in enumerate((ln_scale, ln_offset)):
            raw = const.tile([P, PACK], BF16, name="affine_raw%d" % c)
            nc.scalar.dma_start(out=raw[:], in_=vec.rearrange("(p j) -> p j", j=PACK))
            affine_raw.append(raw)
        w_raw = []
        for o, w in enumerate((wq, wk, wv)):
            w_sb = const.tile([P, PACK, E], BF16, name="w_raw%d" % o)
            nc.sync.dma_start(out=w_sb[:], in_=w.rearrange("(p j) n -> p j n", j=PACK))
            w_raw.append(w_sb)
        rot_raw = []
        for c, table in enumerate((rope_cos, rope_sin)):
            raw = const.tile([P, POS_MACRO, TILES * HALF], BF16, name="rot_raw%d" % c)
            nc.scalar.dma_start(out=raw[:], in_=table.rearrange("(m p i) a -> p m (i a)", p=P, i=TILES))
            rot_raw.append(raw)
        for u in range(LOAD_FIRST, LOAD_AHEAD - STATS_AHEAD):
            load(u)

        one_col = const.tile([P, 1], F32)
        nc.vector.memset(one_col[:], 1.0)
        first_act = const.tile([P, 1], F32)
        nc.scalar.activation(out=first_act[:], in_=one_col[:], func=ACT.Abs_reciprocal_sqrt)
        eps_col = const.tile([P, 1], F32)
        nc.vector.tensor_scalar(out=eps_col[:], in0=one_col[:], scalar1=EPS, scalar2=None, op0=ALU.mult)

        ident = const.tile([P, P], F32)
        make_identity(nc, ident[:])

        affine = const.tile([P, 2 * PACK], F32)
        for c in range(2):
            nc.scalar.copy(out=affine[:, c * PACK : (c + 1) * PACK], in_=affine_raw[c][:])

        rot = const.tile([P, POS_MACRO * TILES, 2, H, ROT], F32)

        HALF_POS = POS_MACRO // 2

        def rotation_views(c, h, half):
            tiles = slice(half * HALF_POS * TILES, (half + 1) * HALF_POS * TILES)
            macros = slice(half * HALF_POS, (half + 1) * HALF_POS)
            return (
                rot[:, tiles, c, h, :].rearrange("p t (a e) -> p t a e", e=2),
                rot_raw[c][:, macros, :]
                .rearrange("p m (i a) -> p (m i) a", a=HALF)
                .unsqueeze(3)
                .to_broadcast([P, HALF_POS * TILES, HALF, 2]),
            )

        def widen_on_gpsimd(c, h, half):
            wide, raw = rotation_views(c, h, half)
            nc.gpsimd.tensor_scalar(out=wide, in0=raw, scalar1=1.0, scalar2=0.0, op0=ALU.mult, op1=ALU.add)

        def widen_on_scalar(c, h, half):
            wide, raw = rotation_views(c, h, half)
            nc.scalar.copy(out=wide, in_=raw)

        w_grouped = const.tile([P, W_COLS, PACK], BF16, align_bytes=64)
        w_codes = const.tile([P, W_COLS], U32, align_bytes=64)
        w_scales = const.tile([P, W_COLS], U8, align_bytes=64)

        def regroup_v_weight():
            nc.gpsimd.tensor_scalar(
                out=w_grouped[:, V_AT : V_AT + V_COLS, :],
                in0=w_raw[2][:].rearrange("p j n -> p n j"),
                scalar1=1.0,
                scalar2=0.0,
                op0=ALU.mult,
                op1=ALU.add,
            )

        def moved(engine, out, in_):
            if engine is nc.scalar:
                nc.scalar.copy(out=out, in_=in_)
            else:
                engine.tensor_copy(out=out, in_=in_)

        def regroup_rope_weight(engine, o):
            by_col = w_raw[o][:].rearrange("p j (h d) -> p h d j", h=H)
            head_cols = H * ROT
            plain_at = ROPE_AT + o * head_cols
            moved(
                engine,
                w_grouped[:, plain_at : plain_at + head_cols, :].rearrange("p (h f) j -> p h f j", h=H),
                by_col[:, :, 0:ROT, :],
            )
            swap_at = ROPE_AT + HEADS_QK * ROT + o * head_cols
            swapped = w_grouped[:, swap_at : swap_at + head_cols, :].rearrange("p (h a e) j -> p h a e j", h=H, e=2)
            pairs = by_col[:, :, 0:ROT, :].rearrange("p h (a e) j -> p h a e j", e=2)
            if engine is nc.scalar:
                nc.scalar.mul(out=swapped[:, :, :, 0, :], in_=pairs[:, :, :, 1, :], mul=-1.0)
            else:
                engine.tensor_scalar(
                    out=swapped[:, :, :, 0, :], in0=pairs[:, :, :, 1, :], scalar1=-1.0, scalar2=None, op0=ALU.mult
                )
            moved(engine, swapped[:, :, :, 1, :], pairs[:, :, :, 0, :])

        def regroup_pass_weight(engine, o):
            by_col = w_raw[o][:].rearrange("p j (h d) -> p h d j", h=H)
            pass_cols = H * (DH - ROT)
            pass_at = PASS_AT + o * pass_cols
            moved(
                engine,
                w_grouped[:, pass_at : pass_at + pass_cols, :].rearrange("p (h d) j -> p h d j", h=H),
                by_col[:, :, ROT:DH, :],
            )

        def quantise_weights():
            for lo, hi in ((0, 512), (512, 768), (768, 896)):
                nc.vector.quantize_mx(
                    out=w_codes[:, lo:hi].bitcast(FP8X4),
                    scales=w_scales[:, lo:hi],
                    in_=w_grouped[:, lo:hi, :].rearrange("p c j -> p (c j)"),
                )

        def token_stats(u, i):
            n = UNITS[u][2]
            if i == 0:
                stats_of[u] = small.tile([P, TILES, 6], F32, name="stats")
            if i < n:
                nc.vector.bn_stats(out=stats_of[u][:, i, :], in_=x_of[u][:, i, :])

        def mean_and_variance(u):
            mean_var_of[u] = small.tile([P, TILES, 2], F32, name="mean_var")
            for i in range(UNITS[u][2]):
                nc.vector.bn_aggr(out=mean_var_of[u][:, i, :], in_=stats_of[u][:, i, :])

        def inverse_std(u):
            n = UNITS[u][2]
            rstd_of[u] = small.tile([P, TILES], F32, name="rstd")
            nc.scalar.activation(
                out=rstd_of[u][:, 0:n], in_=mean_var_of[u][:, 0:n, 1], func=ACT.Abs_reciprocal_sqrt, bias=eps_col[:]
            )

        def negate_mean(u):
            if u in neg_mean_of:
                return
            n = UNITS[u][2]
            neg_mean_of[u] = small.tile([P, TILES], F32, name="neg_mean")
            nc.scalar.mul(out=neg_mean_of[u][:, 0:n], in_=mean_var_of[u][:, 0:n, 0], mul=-1.0)

        def tile_views(u, i):
            if u not in z_of:
                z_of[u] = z_pool.tile([P, TILES, PACK, P], F32, name="z")
            return z_of[u][:, i, :, :], x_of[u][:, i, :].rearrange("p (c j) -> p j c", j=PACK)

        def normalise_on_gpsimd(u):
            for i in range(0 if u < V_HEAD else UNITS[u][2] - 1):
                z, x_tile = tile_views(u, i)
                nc.gpsimd.tensor_scalar(
                    out=z,
                    in0=x_tile,
                    scalar1=neg_mean_of[u][:, i : i + 1],
                    scalar2=rstd_of[u][:, i : i + 1],
                    op0=ALU.add,
                    op1=ALU.mult,
                )

        def normalise_on_vector(u):
            n = UNITS[u][2]
            head = u < V_HEAD
            for i in range(0 if head else n - 1, n):
                z, x_tile = tile_views(u, i)
                lo = 0 if head else SHARE
                nc.vector.tensor_scalar(
                    out=z[:, lo:, :],
                    in0=x_tile[:, lo:, :],
                    scalar1=mean_var_of[u][:, i, 0:1],
                    scalar2=rstd_of[u][:, i : i + 1],
                    op0=ALU.subtract,
                    op1=ALU.mult,
                )

        def normalise_on_scalar(u):
            if u < V_HEAD or SHARE == 0:
                return
            i = UNITS[u][2] - 1
            z, x_tile = tile_views(u, i)
            shift = small.tile([P, 1], F32, name="shift")
            rstd = rstd_of[u][:, i : i + 1]
            nc.scalar.activation(out=shift[:], in_=neg_mean_of[u][:, i : i + 1], func=ACT.Identity, scale=rstd)
            nc.scalar.activation(
                out=z[:, 0:SHARE, :], in_=x_tile[:, 0:SHARE, :], func=ACT.Identity, scale=rstd, bias=shift[:]
            )

        def plane(u, j):
            n = UNITS[u][2]
            return j * n // TILES, j * n % TILES * P

        def transpose(u):
            n = UNITS[u][2]
            planes_ps_of[u] = [bank("plane_ps%d" % b) for b in range(n)]
            for j in range(PACK):
                b, at = plane(u, j)
                for i in range(n):
                    nc.tensor.transpose(
                        planes_ps_of[u][b][:, at + i * P : at + (i + 1) * P], z_of[u][:, i, j, :], ident[:]
                    )

        def scale_shift(u, j):
            n = UNITS[u][2]
            if j == 0:
                planes_of[u] = work.tile([P, PACK, MACRO], BF16, name="xn_planes")
            b, at = plane(u, j)
            nc.scalar.activation(
                out=planes_of[u][:, j, 0 : n * P],
                in_=planes_ps_of[u][b][:, at : at + n * P],
                func=ACT.Identity,
                scale=affine[:, j : j + 1],
                bias=affine[:, PACK + j : PACK + j + 1],
            )

        def regroup(u):
            cols = UNITS[u][2] * P
            grouped_of[u] = work.tile([P, MACRO, PACK], BF16, align_bytes=64, name="xn_grouped")
            nc.vector.tensor_copy(
                out=grouped_of[u][:, 0:cols, :].rearrange("p (c r) j -> p c j r", r=8),
                in_=planes_of[u][:, :, 0:cols].rearrange("p j (c r) -> p c j r", r=8),
            )

        def quantise(u):
            cols = UNITS[u][2] * P
            codes_of[u] = work.tile([P, MACRO], U32, align_bytes=64, name="xn_codes")
            scales_of[u] = work.tile([P, MACRO], U8, align_bytes=64, name="xn_scales")
            nc.vector.quantize_mx(
                out=codes_of[u][:, 0:cols].bitcast(FP8X4),
                scales=scales_of[u][:, 0:cols],
                in_=grouped_of[u][:, 0:cols, :].rearrange("p t j -> p (t j)"),
            )

        def one_pass(u, i, out_ps, at, cols):
            nc.tensor.matmul_mx(
                out=out_ps,
                lhsT=codes_of[u][:, i * P : (i + 1) * P].bitcast(FP8X4),
                lhsT_scale=scales_of[u][:, i * P : (i + 1) * P],
                rhs=w_codes[:, at : at + cols].bitcast(FP8X4),
                rhs_scale=w_scales[:, at : at + cols],
                start=True,
                stop=True,
            )

        def pair_tiles(u, pair):
            return range(2 * pair, min(2 * pair + 2, UNITS[u][2]))

        def project(u, pair):
            tiles = pair_tiles(u, pair)
            if not tiles:
                return
            rope_ps = psum_rope.tile([P, BANK], F32, tag="rope", name="rope_ps")
            v_ps = bank("v_ps")
            pass_ps = [bank("pass_ps%d" % n) for n in range(len(tiles))]
            banks_of[(u, pair)] = (v_ps, pass_ps, rope_ps)
            for n, i in enumerate(tiles):
                one_pass(u, i, rope_ps[:, n * ROPE_COLS : (n + 1) * ROPE_COLS], ROPE_AT, ROPE_COLS)
            for n, i in enumerate(tiles):
                one_pass(u, i, v_ps[:, n * V_COLS : (n + 1) * V_COLS], V_AT, V_COLS)
            for n, i in enumerate(tiles):
                one_pass(u, i, pass_ps[n][:, 0:256], PASS_AT, 256)
                one_pass(u, i, pass_ps[n][:, 256:PASS_COLS], PASS_AT + 256, PASS_COLS - 256)

        def copy_v(u, pair):
            tiles = pair_tiles(u, pair)
            if pair == 0:
                stage_of[u] = out_pool.tile([P, 3, UNITS[u][2], E], F32, name="stage%d" % UNITS[u][2])
            if not tiles:
                return
            v_out = stage_of[u][:, 2, tiles.start : tiles.stop, :].rearrange("p i c -> p (i c)")
            v_in = banks_of[(u, pair)][0][:, 0 : len(tiles) * V_COLS]
            if u < VECTOR_COPY_FROM:
                nc.scalar.copy(out=v_out, in_=v_in)
            else:
                nc.vector.tensor_copy(out=v_out, in_=v_in)

        def copy_pass(u, pair):
            for n, i in enumerate(pair_tiles(u, pair)):
                nc.scalar.copy(
                    out=stage_of[u][:, 0:2, i, :].rearrange("p o (h d) -> p o h d", h=H)[:, :, :, ROT:DH],
                    in_=banks_of[(u, pair)][1][n][:, 0:PASS_COLS].rearrange("p (o h d) -> p o h d", o=2, h=H),
                )

        def rope_products(u, pair):
            m, i0, n = UNITS[u]
            tiles = pair_tiles(u, pair)
            if pair == 0:
                products_of[u] = out_pool.tile([P, 2, n, 2, H * ROT], F32, name="products%d" % n)
            if not tiles:
                return
            v_ps, pass_ps, rope_ps = banks_of[(u, pair)]
            pos = (m % POS_MACRO) * TILES + i0 + tiles.start
            nc.vector.tensor_tensor(
                out=products_of[u][:, :, tiles.start : tiles.stop, :, :].rearrange("p o i c y -> p (i c) o y"),
                in0=rope_ps[:, 0 : len(tiles) * ROPE_COLS].rearrange("p (a o y) -> p a o y", o=2, y=H * ROT),
                in1=rot[:, pos : pos + len(tiles), :, :, :]
                .rearrange("p i c h f -> p (i c) (h f)")
                .unsqueeze(2)
                .to_broadcast([P, 2 * len(tiles), 2, H * ROT]),
                op=ALU.mult,
            )

        def store(u, o):
            m, i0, n = UNITS[u]
            nc.sync.dma_start(
                out=out_rows[o][m][:, i0 * E : (i0 + n) * E], in_=stage_of[u][:, o, :, :].rearrange("p i c -> p (i c)")
            )

        def rotate(u):
            nc.gpsimd.tensor_tensor(
                out=stage_of[u][:, 0:2, :, :].rearrange("p o i (h d) -> p (o i) h d", h=H)[:, :, :, 0:ROT],
                in0=products_of[u][:, :, :, 0, :].rearrange("p o i (h f) -> p (o i) h f", h=H),
                in1=products_of[u][:, :, :, 1, :].rearrange("p o i (h f) -> p (o i) h f", h=H),
                op=ALU.add,
            )

        def when(u, stage, *args):
            if 0 <= u < len(UNITS):
                stage(u, *args)

        for s in range(-STATS_AHEAD, len(UNITS) + 1):
            if s + LOAD_AHEAD >= LOAD_AHEAD - STATS_AHEAD:
                when(s + LOAD_AHEAD, load)
            when(s - 1, rope_products, 1)
            when(s + STATS_AHEAD, token_stats, 0)
            when(s + STATS_AHEAD, token_stats, 1)
            for j in range(PACK):
                when(s + PLANES_AHEAD, scale_shift, j)
            when(s + GPSIMD_AHEAD, normalise_on_gpsimd)
            when(s - 1, rotate)
            when(s - 1, store, 0)
            when(s - 1, store, 1)
            when(s, project, 0)
            when(s, rope_products, 0)
            when(s, copy_v, 0)
            when(s, copy_pass, 0)
            when(s, project, 1)
            when(s + STATS_AHEAD, token_stats, 2)
            when(s + STATS_AHEAD, token_stats, 3)
            when(s + STATS_AHEAD, mean_and_variance)
            if RSTD_AT == 0:
                when(s + STATS_AHEAD, inverse_std)
            if RSTD_AT == 1:
                when(s, copy_v, 1)
                when(s + STATS_AHEAD, inverse_std)
            if RSTD_AT == 2:
                when(s, copy_v, 1)
                when(s, copy_pass, 1)
                when(s + STATS_AHEAD, inverse_std)
            when(s + PLANES_AHEAD, regroup)
            when(s + STATS_AHEAD, normalise_on_vector)
            when(s + PLANES_AHEAD, quantise)
            if RSTD_AT < 1:
                when(s, copy_v, 1)
            if RSTD_AT < 2:
                when(s, copy_pass, 1)
            when(s, store, 2)
            if s + STATS_AHEAD >= V_HEAD:
                when(s + STATS_AHEAD, negate_mean)
            when(s + STATS_AHEAD, normalise_on_scalar)
            when(s + GPSIMD_AHEAD, transpose)
            if s == -3:
                regroup_v_weight()
                regroup_rope_weight(nc.scalar, 0)
                regroup_rope_weight(nc.scalar if WK_ROPE else nc.vector, 1)
                regroup_pass_weight(nc.scalar if WK_PASS else nc.vector, 1)
                widen_on_gpsimd(0, 0, 0)
                widen_on_gpsimd(1, 0, 0)
            elif s == -2:
                regroup_pass_weight(nc.scalar, 0)
                quantise_weights()
                widen_on_scalar(0, 1, 0)
                widen_on_scalar(1, 1, 0)
            elif 1 <= s <= 4:
                widen_on_scalar((s - 1) // 2, (s - 1) % 2, 1)
